import numpy as np
import ml_dtypes

BF16 = ml_dtypes.bfloat16


def bf(x):
    return np.asarray(x, np.float32).astype(BF16)


def f32(x):
    return np.asarray(x, np.float32)


def f64(x):
    return np.asarray(x).astype(np.float64)


def striped(idx):
    return np.tile(idx.reshape(-1, 16).T, (8, 1))


S, D, M, N = 256, 128, 128, 128
SCALE = 1.0 / np.sqrt(D)


def setup_inputs():
    return {
        "table": bf(np.random.standard_normal((S, D))),
        "kscale": f32(0.4 + 1.4 * np.random.uniform(size=(S, 1))),
        "q": bf(np.random.standard_normal((D, M))),
        "v": bf(np.random.standard_normal((N, D))),
        "vscale": f32(0.4 + 1.4 * np.random.uniform(size=(N, 1))),
        "offs": striped(np.random.permutation(S)[:N]),
    }


def reference(table, kscale, q, v, vscale, offs):
    idx = offs[:16].T.reshape(-1)
    kd = f64(table) * f64(kscale)
    sc = SCALE * (f64(q).T @ kd[idx].T)
    e = np.exp(sc - sc.max(axis=1, keepdims=True))
    vd = f64(v) * f64(vscale)
    return (e @ vd) / e.sum(axis=1, keepdims=True)

@@ -1,0 +1,72 @@
+import math
+
+import concourse.mybir as mybir
+from concourse.masks import make_identity
+
+P = 128
+S = 256
+N = 128
+BLOCKS = S // P
+SCALE = 1.0 / math.sqrt(P)
+FLOPS = 2 * (2 * P * N * P)
+
+BF16, F32, U16 = mybir.dt.bfloat16, mybir.dt.float32, mybir.dt.uint16
+MULT = mybir.AluOpType.mult
+EXP, COPY = mybir.ActivationFunctionType.Exp, mybir.ActivationFunctionType.Copy
+X = mybir.AxisListType.X
+
+
+def tile_sfaanetwork_kernel(tc, table, kscale, q, v, vscale, offs, out):
+    nc = tc.nc
+    with tc.tile_pool(name="held", bufs=1) as held, tc.psum_pool(name="psum", bufs=1) as psum:
+        raw_keys = [held.tile([P, P], BF16, name=f"raw_keys{b}") for b in range(BLOCKS)]
+        key_scales = held.tile([P, S], F32, name="key_scales")
+        offsets = held.tile([P, N // 16], U16, name="offsets")
+        queries = held.tile([P, P], BF16, name="queries")
+        raw_values = held.tile([P, P], BF16, name="raw_values")
+        value_scales = held.tile([P, 1], F32, name="value_scales")
+
+        nc.sync.dma_start(raw_keys[0][:], table[0:P, :])
+        nc.scalar.dma_start(key_scales[:], kscale.rearrange("t o -> (t o)").partition_broadcast(P))
+        nc.sync.dma_start(raw_keys[1][:], table[P:S, :])
+        nc.sync.dma_start(offsets[:], offs)
+        nc.scalar.dma_start(queries[:], q)
+        nc.gpsimd.dma_start(raw_values[:], v)
+        nc.gpsimd.dma_start(value_scales[:], vscale)
+
+        identity = held.tile([P, P], BF16, name="identity")
+        make_identity(nc, identity[:])
+
+        keys = held.tile([P, S], BF16, name="keys")
+        for b in range(BLOCKS):
+            flipped_keys = psum.tile([P, P], BF16, name=f"flipped_keys{b}")
+            nc.tensor.transpose(flipped_keys[:], raw_keys[b][:], identity[:])
+            block = slice(b * P, (b + 1) * P)
+            nc.vector.tensor_tensor(keys[:, block], flipped_keys[:], key_scales[:, block], MULT)
+
+        values = held.tile([P, P], BF16, name="values")
+        nc.scalar.activation(values[:], raw_values[:], COPY, scale=value_scales[:, 0:1])
+
+        scores = psum.tile([P, N], F32, name="scores")
+        nc.tensor.matmul(scores[:], queries[:], keys[:].indirect(offsets[:]), start=True, stop=True)
+
+        top = held.tile([P, 1], F32, name="top")
+        nc.vector.reduce_max(top[:], scores[:], axis=X)
+        shift = held.tile([P, 1], F32, name="shift")
+        nc.vector.tensor_scalar(shift[:], top[:], -SCALE, None, MULT)
+        weights = held.tile([P, N], BF16, name="weights")
+        z = held.tile([P, 1], F32, name="z")
+        nc.scalar.activation(weights[:], scores[:], EXP, bias=shift[:, 0:1], scale=SCALE, accum_out=z[:])
+        inverse_z = held.tile([P, 1], F32, name="inverse_z")
+        nc.vector.reciprocal(inverse_z[:], z[:])
+
+        flipped_weights_psum = psum.tile([P, P], BF16, name="flipped_weights_psum")
+        nc.tensor.transpose(flipped_weights_psum[:], weights[:], identity[:])
+        flipped_weights = held.tile([P, P], BF16, name="flipped_weights")
+        nc.vector.tensor_copy(flipped_weights[:], flipped_weights_psum[:])
+        mixed = psum.tile([P, P], F32, name="mixed")
+        nc.tensor.matmul(mixed[:], flipped_weights[:], values[:], start=True, stop=True)
+
+        result = held.tile([P, P], F32, name="result")
+        nc.vector.tensor_scalar(result[:], mixed[:], inverse_z[:, 0:1], None, MULT)
+        nc.sync.dma_start(out, result[:])

@@ -37,6 +37,10 @@ def tile_sfaanetwork_kernel(tc, table, kscale, q, v, vscale, offs, out):
         identity = held.tile([P, P], BF16, name="identity")
         make_identity(nc, identity[:])
 
+        scratch = held.tile([P, 1], F32, name="scratch")
+        nc.vector.memset(scratch[:], 0.0)
+        nc.scalar.activation(scratch[:], scratch[:], EXP)
+
         keys = held.tile([P, S], BF16, name="keys")
         for b in range(BLOCKS):
             flipped_keys = psum.tile([P, P], BF16, name=f"flipped_keys{b}")

@@ -12,7 +12,7 @@ FLOPS = 2 * (2 * P * N * P)
 
 BF16, F32, U16 = mybir.dt.bfloat16, mybir.dt.float32, mybir.dt.uint16
 MULT = mybir.AluOpType.mult
-EXP, COPY = mybir.ActivationFunctionType.Exp, mybir.ActivationFunctionType.Copy
+EXP = mybir.ActivationFunctionType.Exp
 X = mybir.AxisListType.X
 
 
@@ -29,10 +29,10 @@ def tile_sfaanetwork_kernel(tc, table, kscale, q, v, vscale, offs, out):
         nc.sync.dma_start(raw_keys[0][:], table[0:P, :])
         nc.scalar.dma_start(key_scales[:], kscale.rearrange("t o -> (t o)").partition_broadcast(P))
         nc.sync.dma_start(raw_keys[1][:], table[P:S, :])
-        nc.sync.dma_start(offsets[:], offs)
         nc.scalar.dma_start(queries[:], q)
-        nc.gpsimd.dma_start(raw_values[:], v)
-        nc.gpsimd.dma_start(value_scales[:], vscale)
+        nc.sync.dma_start(offsets[:], offs)
+        nc.scalar.dma_start(value_scales[:], vscale)
+        nc.sync.dma_start(raw_values[:], v)
 
         identity = held.tile([P, P], BF16, name="identity")
         make_identity(nc, identity[:])
@@ -49,7 +49,7 @@ def tile_sfaanetwork_kernel(tc, table, kscale, q, v, vscale, offs, out):
             nc.vector.tensor_tensor(keys[:, block], flipped_keys[:], key_scales[:, block], MULT)
 
         values = held.tile([P, P], BF16, name="values")
-        nc.scalar.activation(values[:], raw_values[:], COPY, scale=value_scales[:, 0:1])
+        nc.gpsimd.tensor_scalar(values[:], raw_values[:], value_scales[:, 0:1], None, MULT)
 
         scores = psum.tile([P, N], F32, name="scores")
         nc.tensor.matmul(scores[:], queries[:], keys[:].indirect(offsets[:]), start=True, stop=True)

@@ -12,7 +12,7 @@ FLOPS = 2 * (2 * P * N * P)
 
 BF16, F32, U16 = mybir.dt.bfloat16, mybir.dt.float32, mybir.dt.uint16
 MULT = mybir.AluOpType.mult
-EXP = mybir.ActivationFunctionType.Exp
+EXP, COPY = mybir.ActivationFunctionType.Exp, mybir.ActivationFunctionType.Copy
 X = mybir.AxisListType.X
 
 
@@ -20,15 +20,16 @@ def tile_sfaanetwork_kernel(tc, table, kscale, q, v, vscale, offs, out):
     nc = tc.nc
     with tc.tile_pool(name="held", bufs=1) as held, tc.psum_pool(name="psum", bufs=1) as psum:
         raw_keys = [held.tile([P, P], BF16, name=f"raw_keys{b}") for b in range(BLOCKS)]
-        key_scales = held.tile([P, S], F32, name="key_scales")
+        key_scales = held.tile([P, BLOCKS], F32, name="key_scales")
         offsets = held.tile([P, N // 16], U16, name="offsets")
         queries = held.tile([P, P], BF16, name="queries")
         raw_values = held.tile([P, P], BF16, name="raw_values")
         value_scales = held.tile([P, 1], F32, name="value_scales")
 
+        with nc.allow_non_contiguous_dma(reason="one float32 scale for each token's partition"):
+            nc.sync.dma_start(key_scales[:], kscale.rearrange("(b p) o -> p (b o)", p=P))
+        nc.scalar.dma_start(raw_keys[1][:], table[P:S, :])
         nc.sync.dma_start(raw_keys[0][:], table[0:P, :])
-        nc.scalar.dma_start(key_scales[:], kscale.rearrange("t o -> (t o)").partition_broadcast(P))
-        nc.sync.dma_start(raw_keys[1][:], table[P:S, :])
         nc.scalar.dma_start(queries[:], q)
         nc.sync.dma_start(offsets[:], offs)
         nc.scalar.dma_start(value_scales[:], vscale)
@@ -42,11 +43,14 @@ def tile_sfaanetwork_kernel(tc, table, kscale, q, v, vscale, offs, out):
         nc.scalar.activation(scratch[:], scratch[:], EXP)
 
         keys = held.tile([P, S], BF16, name="keys")
+        scaled_keys = [held.tile([P, P], BF16, name=f"scaled_keys{b}") for b in range(BLOCKS)]
+        flipped_keys = [psum.tile([P, P], BF16, name=f"flipped_keys{b}") for b in range(BLOCKS)]
+        nc.vector.tensor_scalar(scaled_keys[0][:], raw_keys[0][:], key_scales[:, 0:1], None, MULT)
+        nc.scalar.activation(scaled_keys[1][:], raw_keys[1][:], COPY, scale=key_scales[:, 1:2])
         for b in range(BLOCKS):
-            flipped_keys = psum.tile([P, P], BF16, name=f"flipped_keys{b}")
-            nc.tensor.transpose(flipped_keys[:], raw_keys[b][:], identity[:])
-            block = slice(b * P, (b + 1) * P)
-            nc.vector.tensor_tensor(keys[:, block], flipped_keys[:], key_scales[:, block], MULT)
+            nc.tensor.transpose(flipped_keys[b][:], scaled_keys[b][:], identity[:])
+        nc.vector.tensor_copy(keys[:, 0:P], flipped_keys[0][:])
+        nc.scalar.copy(keys[:, P:S], flipped_keys[1][:])
 
         values = held.tile([P, P], BF16, name="values")
         nc.gpsimd.tensor_scalar(values[:], raw_values[:], value_scales[:, 0:1], None, MULT)

@@ -11,9 +11,8 @@ SCALE = 1.0 / math.sqrt(P)
 FLOPS = 2 * (2 * P * N * P)
 
 BF16, F32, U16 = mybir.dt.bfloat16, mybir.dt.float32, mybir.dt.uint16
-MULT = mybir.AluOpType.mult
+MULT, MIN = mybir.AluOpType.mult, mybir.AluOpType.min
 EXP, COPY = mybir.ActivationFunctionType.Exp, mybir.ActivationFunctionType.Copy
-X = mybir.AxisListType.X
 
 
 def tile_sfaanetwork_kernel(tc, table, kscale, q, v, vscale, offs, out):
@@ -58,10 +57,9 @@ def tile_sfaanetwork_kernel(tc, table, kscale, q, v, vscale, offs, out):
         scores = psum.tile([P, N], F32, name="scores")
         nc.tensor.matmul(scores[:], queries[:], keys[:].indirect(offsets[:]), start=True, stop=True)
 
-        top = held.tile([P, 1], F32, name="top")
-        nc.vector.reduce_max(top[:], scores[:], axis=X)
+        negated = held.tile([P, N], F32, name="negated")
         shift = held.tile([P, 1], F32, name="shift")
-        nc.vector.tensor_scalar(shift[:], top[:], -SCALE, None, MULT)
+        nc.vector.tensor_scalar(negated[:], scores[:], -SCALE, None, MULT, MIN, accum_out=shift[:])
         weights = held.tile([P, N], BF16, name="weights")
         z = held.tile([P, 1], F32, name="z")
         nc.scalar.activation(weights[:], scores[:], EXP, bias=shift[:, 0:1], scale=SCALE, accum_out=z[:])

@@ -12,7 +12,7 @@ FLOPS = 2 * (2 * P * N * P)
 
 BF16, F32, U16 = mybir.dt.bfloat16, mybir.dt.float32, mybir.dt.uint16
 MULT, MIN = mybir.AluOpType.mult, mybir.AluOpType.min
-EXP, COPY = mybir.ActivationFunctionType.Exp, mybir.ActivationFunctionType.Copy
+EXP = mybir.ActivationFunctionType.Exp
 
 
 def tile_sfaanetwork_kernel(tc, table, kscale, q, v, vscale, offs, out):
@@ -25,10 +25,10 @@ def tile_sfaanetwork_kernel(tc, table, kscale, q, v, vscale, offs, out):
         raw_values = held.tile([P, P], BF16, name="raw_values")
         value_scales = held.tile([P, 1], F32, name="value_scales")
 
-        with nc.allow_non_contiguous_dma(reason="one float32 scale for each token's partition"):
-            nc.sync.dma_start(key_scales[:], kscale.rearrange("(b p) o -> p (b o)", p=P))
-        nc.scalar.dma_start(raw_keys[1][:], table[P:S, :])
         nc.sync.dma_start(raw_keys[0][:], table[0:P, :])
+        with nc.allow_non_contiguous_dma(reason="one float32 scale for each token's partition"):
+            nc.scalar.dma_start(key_scales[:], kscale.rearrange("(b p) o -> p (b o)", p=P))
+        nc.sync.dma_start(raw_keys[1][:], table[P:S, :])
         nc.scalar.dma_start(queries[:], q)
         nc.sync.dma_start(offsets[:], offs)
         nc.scalar.dma_start(value_scales[:], vscale)
@@ -42,14 +42,12 @@ def tile_sfaanetwork_kernel(tc, table, kscale, q, v, vscale, offs, out):
         nc.scalar.activation(scratch[:], scratch[:], EXP)
 
         keys = held.tile([P, S], BF16, name="keys")
-        scaled_keys = [held.tile([P, P], BF16, name=f"scaled_keys{b}") for b in range(BLOCKS)]
-        flipped_keys = [psum.tile([P, P], BF16, name=f"flipped_keys{b}") for b in range(BLOCKS)]
-        nc.vector.tensor_scalar(scaled_keys[0][:], raw_keys[0][:], key_scales[:, 0:1], None, MULT)
-        nc.scalar.activation(scaled_keys[1][:], raw_keys[1][:], COPY, scale=key_scales[:, 1:2])
         for b in range(BLOCKS):
-            nc.tensor.transpose(flipped_keys[b][:], scaled_keys[b][:], identity[:])
-        nc.vector.tensor_copy(keys[:, 0:P], flipped_keys[0][:])
-        nc.scalar.copy(keys[:, P:S], flipped_keys[1][:])
+            scaled_keys = held.tile([P, P], BF16, name=f"scaled_keys{b}")
+            nc.vector.tensor_scalar(scaled_keys[:], raw_keys[b][:], key_scales[:, b : b + 1], None, MULT)
+            flipped_keys = psum.tile([P, P], BF16, name=f"flipped_keys{b}")
+            nc.tensor.transpose(flipped_keys[:], scaled_keys[:], identity[:])
+            nc.vector.tensor_copy(keys[:, b * P : (b + 1) * P], flipped_keys[:])
 
         values = held.tile([P, P], BF16, name="values")
         nc.gpsimd.tensor_scalar(values[:], raw_values[:], value_scales[:, 0:1], None, MULT)

@@ -8,6 +8,7 @@ S = 256
 N = 128
 BLOCKS = S // P
 SCALE = 1.0 / math.sqrt(P)
+FILL_LOADS = 16
 FLOPS = 2 * (2 * P * N * P)
 
 BF16, F32, U16 = mybir.dt.bfloat16, mybir.dt.float32, mybir.dt.uint16
@@ -33,6 +34,12 @@ def tile_sfaanetwork_kernel(tc, table, kscale, q, v, vscale, offs, out):
         nc.sync.dma_start(offsets[:], offs)
         nc.scalar.dma_start(value_scales[:], vscale)
         nc.sync.dma_start(raw_values[:], v)
+
+        zeros = held.tile([P, P], BF16, name="zeros")
+        nc.gpsimd.memset(zeros[:], 0.0)
+        unread = psum.tile([P, P], F32, name="unread")
+        for i in range(FILL_LOADS):
+            nc.tensor.matmul(unread[:], zeros[:], zeros[:], start=True, stop=True)
 
         identity = held.tile([P, P], BF16, name="identity")
         make_identity(nc, identity[:])

@@ -19,17 +19,15 @@ EXP = mybir.ActivationFunctionType.Exp
 def tile_sfaanetwork_kernel(tc, table, kscale, q, v, vscale, offs, out):
     nc = tc.nc
     with tc.tile_pool(name="held", bufs=1) as held, tc.psum_pool(name="psum", bufs=1) as psum:
-        raw_keys = [held.tile([P, P], BF16, name=f"raw_keys{b}") for b in range(BLOCKS)]
+        raw_keys = held.tile([P, BLOCKS * P], BF16, name="raw_keys")
         key_scales = held.tile([P, BLOCKS], F32, name="key_scales")
         offsets = held.tile([P, N // 16], U16, name="offsets")
         queries = held.tile([P, P], BF16, name="queries")
         raw_values = held.tile([P, P], BF16, name="raw_values")
         value_scales = held.tile([P, 1], F32, name="value_scales")
 
-        nc.sync.dma_start(raw_keys[0][:], table[0:P, :])
-        with nc.allow_non_contiguous_dma(reason="one float32 scale for each token's partition"):
-            nc.scalar.dma_start(key_scales[:], kscale.rearrange("(b p) o -> p (b o)", p=P))
-        nc.sync.dma_start(raw_keys[1][:], table[P:S, :])
+        nc.sync.dma_start(raw_keys[:], table.rearrange("(p b) d -> p (b d)", b=BLOCKS))
+        nc.scalar.dma_start(key_scales[:], kscale.rearrange("(p b) o -> p (b o)", b=BLOCKS))
         nc.scalar.dma_start(queries[:], q)
         nc.sync.dma_start(offsets[:], offs)
         nc.scalar.dma_start(value_scales[:], vscale)
@@ -49,12 +47,16 @@ def tile_sfaanetwork_kernel(tc, table, kscale, q, v, vscale, offs, out):
         nc.scalar.activation(scratch[:], scratch[:], EXP)
 
         keys = held.tile([P, S], BF16, name="keys")
+        flipped_keys = psum.tile([P, S], BF16, name="flipped_keys")
         for b in range(BLOCKS):
+            block = slice(b * P, (b + 1) * P)
             scaled_keys = held.tile([P, P], BF16, name=f"scaled_keys{b}")
-            nc.vector.tensor_scalar(scaled_keys[:], raw_keys[b][:], key_scales[:, b : b + 1], None, MULT)
-            flipped_keys = psum.tile([P, P], BF16, name=f"flipped_keys{b}")
-            nc.tensor.transpose(flipped_keys[:], scaled_keys[:], identity[:])
-            nc.vector.tensor_copy(keys[:, b * P : (b + 1) * P], flipped_keys[:])
+            nc.vector.tensor_scalar(scaled_keys[:], raw_keys[:, block], key_scales[:, b : b + 1], None, MULT)
+            nc.tensor.transpose(flipped_keys[:, block], scaled_keys[:], identity[:])
+        nc.vector.tensor_copy(
+            keys[:].rearrange("d (p b) -> d p b", b=BLOCKS),
+            flipped_keys[:].rearrange("d (b p) -> d p b", b=BLOCKS),
+        )
 
         values = held.tile([P, P], BF16, name="values")
         nc.gpsimd.tensor_scalar(values[:], raw_values[:], value_scales[:, 0:1], None, MULT)

@@ -9,6 +9,9 @@ N = 128
 BLOCKS = S // P
 SCALE = 1.0 / math.sqrt(P)
 FILL_LOADS = 16
+FILL_WINDOW = 3
+FILL_SOFTMAX = 6
+FILL_WEIGHTS = 2
 FLOPS = 2 * (2 * P * N * P)
 
 BF16, F32, U16 = mybir.dt.bfloat16, mybir.dt.float32, mybir.dt.uint16
@@ -39,6 +42,10 @@ def tile_sfaanetwork_kernel(tc, table, kscale, q, v, vscale, offs, out):
         for i in range(FILL_LOADS):
             nc.tensor.matmul(unread[:], zeros[:], zeros[:], start=True, stop=True)
 
+        def keep_busy(count, just_made):
+            for i in range(count):
+                nc.tensor.matmul(unread[:], just_made, zeros[:], start=True, stop=True)
+
         identity = held.tile([P, P], BF16, name="identity")
         make_identity(nc, identity[:])
 
@@ -53,6 +60,7 @@ def tile_sfaanetwork_kernel(tc, table, kscale, q, v, vscale, offs, out):
             scaled_keys = held.tile([P, P], BF16, name=f"scaled_keys{b}")
             nc.vector.tensor_scalar(scaled_keys[:], raw_keys[:, block], key_scales[:, b : b + 1], None, MULT)
             nc.tensor.transpose(flipped_keys[:, block], scaled_keys[:], identity[:])
+        keep_busy(FILL_WINDOW, scaled_keys[:])
         nc.vector.tensor_copy(
             keys[:].rearrange("d (p b) -> d p b", b=BLOCKS),
             flipped_keys[:].rearrange("d (b p) -> d p b", b=BLOCKS),
@@ -63,6 +71,7 @@ def tile_sfaanetwork_kernel(tc, table, kscale, q, v, vscale, offs, out):
 
         scores = psum.tile([P, N], F32, name="scores")
         nc.tensor.matmul(scores[:], queries[:], keys[:].indirect(offsets[:]), start=True, stop=True)
+        keep_busy(FILL_SOFTMAX, keys[:, 0:P])
 
         negated = held.tile([P, N], F32, name="negated")
         shift = held.tile([P, 1], F32, name="shift")
@@ -75,6 +84,7 @@ def tile_sfaanetwork_kernel(tc, table, kscale, q, v, vscale, offs, out):
 
         flipped_weights_psum = psum.tile([P, P], BF16, name="flipped_weights_psum")
         nc.tensor.transpose(flipped_weights_psum[:], weights[:], identity[:])
+        keep_busy(FILL_WEIGHTS, weights[:])
         flipped_weights = held.tile([P, P], BF16, name="flipped_weights")
         nc.vector.tensor_copy(flipped_weights[:], flipped_weights_psum[:])
         mixed = psum.tile([P, P], F32, name="mixed")

@@ -9,9 +9,7 @@ N = 128
 BLOCKS = S // P
 SCALE = 1.0 / math.sqrt(P)
 FILL_LOADS = 16
-FILL_WINDOW = 3
 FILL_SOFTMAX = 6
-FILL_WEIGHTS = 2
 FLOPS = 2 * (2 * P * N * P)
 
 BF16, F32, U16 = mybir.dt.bfloat16, mybir.dt.float32, mybir.dt.uint16
@@ -60,7 +58,6 @@ def tile_sfaanetwork_kernel(tc, table, kscale, q, v, vscale, offs, out):
             scaled_keys = held.tile([P, P], BF16, name=f"scaled_keys{b}")
             nc.vector.tensor_scalar(scaled_keys[:], raw_keys[:, block], key_scales[:, b : b + 1], None, MULT)
             nc.tensor.transpose(flipped_keys[:, block], scaled_keys[:], identity[:])
-        keep_busy(FILL_WINDOW, scaled_keys[:])
         nc.vector.tensor_copy(
             keys[:].rearrange("d (p b) -> d p b", b=BLOCKS),
             flipped_keys[:].rearrange("d (b p) -> d p b", b=BLOCKS),
@@ -84,7 +81,6 @@ def tile_sfaanetwork_kernel(tc, table, kscale, q, v, vscale, offs, out):
 
         flipped_weights_psum = psum.tile([P, P], BF16, name="flipped_weights_psum")
         nc.tensor.transpose(flipped_weights_psum[:], weights[:], identity[:])
-        keep_busy(FILL_WEIGHTS, weights[:])
         flipped_weights = held.tile([P, P], BF16, name="flipped_weights")
         nc.vector.tensor_copy(flipped_weights[:], flipped_weights_psum[:])
         mixed = psum.tile([P, P], F32, name="mixed")

@@ -8,7 +8,7 @@ S = 256
 N = 128
 BLOCKS = S // P
 SCALE = 1.0 / math.sqrt(P)
-FILL_LOADS = 16
+FILL_LOADS = 13
 FILL_SOFTMAX = 6
 FLOPS = 2 * (2 * P * N * P)
 

@@ -8,8 +8,8 @@ S = 256
 N = 128
 BLOCKS = S // P
 SCALE = 1.0 / math.sqrt(P)
-FILL_LOADS = 13
-FILL_SOFTMAX = 6
+FILL_LOADS = 14
+FILL_SOFTMAX = 8
 FLOPS = 2 * (2 * P * N * P)
 
 BF16, F32, U16 = mybir.dt.bfloat16, mybir.dt.float32, mybir.dt.uint16

@@ -34,22 +34,22 @@ def tile_sfaanetwork_kernel(tc, table, kscale, q, v, vscale, offs, out):
         nc.scalar.dma_start(value_scales[:], vscale)
         nc.sync.dma_start(raw_values[:], v)
 
-        zeros = held.tile([P, P], BF16, name="zeros")
-        nc.gpsimd.memset(zeros[:], 0.0)
+        zero = held.tile([P, 2], BF16, name="zero")
+        nc.vector.memset(zero[:], 0.0)
+        zeros = zero[:, 0:1].to_broadcast([P, P])
         unread = psum.tile([P, P], F32, name="unread")
         for i in range(FILL_LOADS):
-            nc.tensor.matmul(unread[:], zeros[:], zeros[:], start=True, stop=True)
+            nc.tensor.matmul(unread[:], zeros, zeros, start=True, stop=True)
 
         def keep_busy(count, just_made):
             for i in range(count):
-                nc.tensor.matmul(unread[:], just_made, zeros[:], start=True, stop=True)
+                nc.tensor.matmul(unread[:], just_made, zeros, start=True, stop=True)
 
         identity = held.tile([P, P], BF16, name="identity")
         make_identity(nc, identity[:])
 
         scratch = held.tile([P, 1], F32, name="scratch")
-        nc.vector.memset(scratch[:], 0.0)
-        nc.scalar.activation(scratch[:], scratch[:], EXP)
+        nc.scalar.activation(scratch[:], zero[:, 0:1], EXP)
 
         keys = held.tile([P, S], BF16, name="keys")
         flipped_keys = psum.tile([P, S], BF16, name="flipped_keys")

@@ -27,8 +27,8 @@ def tile_sfaanetwork_kernel(tc, table, kscale, q, v, vscale, offs, out):
         raw_values = held.tile([P, P], BF16, name="raw_values")
         value_scales = held.tile([P, 1], F32, name="value_scales")
 
-        nc.sync.dma_start(raw_keys[:], table.rearrange("(p b) d -> p (b d)", b=BLOCKS))
-        nc.scalar.dma_start(key_scales[:], kscale.rearrange("(p b) o -> p (b o)", b=BLOCKS))
+        nc.sync.dma_start(key_scales[:], kscale.rearrange("(p b) o -> p (b o)", b=BLOCKS))
+        nc.scalar.dma_start(raw_keys[:], table.rearrange("(p b) d -> p (b d)", b=BLOCKS))
         nc.scalar.dma_start(queries[:], q)
         nc.sync.dma_start(offsets[:], offs)
         nc.scalar.dma_start(value_scales[:], vscale)

@@ -29,9 +29,9 @@ def tile_sfaanetwork_kernel(tc, table, kscale, q, v, vscale, offs, out):
 
         nc.sync.dma_start(key_scales[:], kscale.rearrange("(p b) o -> p (b o)", b=BLOCKS))
         nc.scalar.dma_start(raw_keys[:], table.rearrange("(p b) d -> p (b d)", b=BLOCKS))
-        nc.scalar.dma_start(queries[:], q)
         nc.sync.dma_start(offsets[:], offs)
-        nc.scalar.dma_start(value_scales[:], vscale)
+        nc.sync.dma_start(queries[:], q)
+        nc.sync.dma_start(value_scales[:], vscale)
         nc.sync.dma_start(raw_values[:], v)
 
         zero = held.tile([P, 2], BF16, name="zero")

@@ -8,7 +8,7 @@ S = 256
 N = 128
 BLOCKS = S // P
 SCALE = 1.0 / math.sqrt(P)
-FILL_LOADS = 14
+FILL_LOADS = 15
 FILL_SOFTMAX = 8
 FLOPS = 2 * (2 * P * N * P)
 
@@ -35,7 +35,7 @@ def tile_sfaanetwork_kernel(tc, table, kscale, q, v, vscale, offs, out):
         nc.sync.dma_start(raw_values[:], v)
 
         zero = held.tile([P, 2], BF16, name="zero")
-        nc.vector.memset(zero[:], 0.0)
+        nc.gpsimd.memset(zero[:], 0.0)
         zeros = zero[:, 0:1].to_broadcast([P, P])
         unread = psum.tile([P, P], F32, name="unread")
         for i in range(FILL_LOADS):

import math

import concourse.mybir as mybir
from concourse.masks import make_identity

P = 128
S = 256
N = 128
BLOCKS = S // P
SCALE = 1.0 / math.sqrt(P)
FILL_LOADS = 15
FILL_SOFTMAX = 8
FLOPS = 2 * (2 * P * N * P)

BF16, F32, U16 = mybir.dt.bfloat16, mybir.dt.float32, mybir.dt.uint16
MULT, MIN = mybir.AluOpType.mult, mybir.AluOpType.min
EXP = mybir.ActivationFunctionType.Exp


def tile_sfaanetwork_kernel(tc, table, kscale, q, v, vscale, offs, out):
    nc = tc.nc
    with tc.tile_pool(name="held", bufs=1) as held, tc.psum_pool(name="psum", bufs=1) as psum:
        raw_keys = held.tile([P, BLOCKS * P], BF16, name="raw_keys")
        key_scales = held.tile([P, BLOCKS], F32, name="key_scales")
        offsets = held.tile([P, N // 16], U16, name="offsets")
        queries = held.tile([P, P], BF16, name="queries")
        raw_values = held.tile([P, P], BF16, name="raw_values")
        value_scales = held.tile([P, 1], F32, name="value_scales")

        nc.sync.dma_start(key_scales[:], kscale.rearrange("(p b) o -> p (b o)", b=BLOCKS))
        nc.scalar.dma_start(raw_keys[:], table.rearrange("(p b) d -> p (b d)", b=BLOCKS))
        nc.sync.dma_start(offsets[:], offs)
        nc.sync.dma_start(queries[:], q)
        nc.sync.dma_start(value_scales[:], vscale)
        nc.sync.dma_start(raw_values[:], v)

        zero = held.tile([P, 2], BF16, name="zero")
        nc.gpsimd.memset(zero[:], 0.0)
        zeros = zero[:, 0:1].to_broadcast([P, P])
        unread = psum.tile([P, P], F32, name="unread")
        for i in range(FILL_LOADS):
            nc.tensor.matmul(unread[:], zeros, zeros, start=True, stop=True)

        def keep_busy(count, just_made):
            for i in range(count):
                nc.tensor.matmul(unread[:], just_made, zeros, start=True, stop=True)

        identity = held.tile([P, P], BF16, name="identity")
        make_identity(nc, identity[:])

        scratch = held.tile([P, 1], F32, name="scratch")
        nc.scalar.activation(scratch[:], zero[:, 0:1], EXP)

        keys = held.tile([P, S], BF16, name="keys")
        flipped_keys = psum.tile([P, S], BF16, name="flipped_keys")
        for b in range(BLOCKS):
            block = slice(b * P, (b + 1) * P)
            scaled_keys = held.tile([P, P], BF16, name=f"scaled_keys{b}")
            nc.vector.tensor_scalar(scaled_keys[:], raw_keys[:, block], key_scales[:, b : b + 1], None, MULT)
            nc.tensor.transpose(flipped_keys[:, block], scaled_keys[:], identity[:])
        nc.vector.tensor_copy(
            keys[:].rearrange("d (p b) -> d p b", b=BLOCKS),
            flipped_keys[:].rearrange("d (b p) -> d p b", b=BLOCKS),
        )

        values = held.tile([P, P], BF16, name="values")
        nc.gpsimd.tensor_scalar(values[:], raw_values[:], value_scales[:, 0:1], None, MULT)

        scores = psum.tile([P, N], F32, name="scores")
        nc.tensor.matmul(scores[:], queries[:], keys[:].indirect(offsets[:]), start=True, stop=True)
        keep_busy(FILL_SOFTMAX, keys[:, 0:P])

        negated = held.tile([P, N], F32, name="negated")
        shift = held.tile([P, 1], F32, name="shift")
        nc.vector.tensor_scalar(negated[:], scores[:], -SCALE, None, MULT, MIN, accum_out=shift[:])
        weights = held.tile([P, N], BF16, name="weights")
        z = held.tile([P, 1], F32, name="z")
        nc.scalar.activation(weights[:], scores[:], EXP, bias=shift[:, 0:1], scale=SCALE, accum_out=z[:])
        inverse_z = held.tile([P, 1], F32, name="inverse_z")
        nc.vector.reciprocal(inverse_z[:], z[:])

        flipped_weights_psum = psum.tile([P, P], BF16, name="flipped_weights_psum")
        nc.tensor.transpose(flipped_weights_psum[:], weights[:], identity[:])
        flipped_weights = held.tile([P, P], BF16, name="flipped_weights")
        nc.vector.tensor_copy(flipped_weights[:], flipped_weights_psum[:])
        mixed = psum.tile([P, P], F32, name="mixed")
        nc.tensor.matmul(mixed[:], flipped_weights[:], values[:], start=True, stop=True)

        result = held.tile([P, P], F32, name="result")
        nc.vector.tensor_scalar(result[:], mixed[:], inverse_z[:, 0:1], None, MULT)
        nc.sync.dma_start(out, result[:])
